import numpy as np
import ml_dtypes


def mxq(x, axis, fmt="e4m3"):
    dtype, down = {"e4m3": (ml_dtypes.float8_e4m3fn, 7), "e5m2": (ml_dtypes.float8_e5m2, 14)}[fmt]
    v = np.moveaxis(np.asarray(x, np.float32).astype(ml_dtypes.bfloat16).astype(np.float64), axis, -1)
    blocks = v.reshape(v.shape[:-1] + (-1, 32))
    amax = np.abs(blocks).max(-1, keepdims=True)
    byte = np.maximum(np.where(amax > 0, np.frexp(amax)[1] - 1 + 127, 0) - down, 1)
    scale = np.exp2(byte - 127.0)
    codes = (blocks / scale).astype(np.float32).astype(dtype).astype(np.float64)
    return np.moveaxis((codes * scale).reshape(v.shape), -1, axis)


WIDE = False


def mx_kscale(k):
    if not WIDE:
        return np.ones(k)
    levels = np.array([30, -30])
    if k % 512:
        return np.exp2(np.random.permutation(np.resize(levels, k // 32))).repeat(32)
    a = np.empty((k // 512, 16))
    for p in range(k // 512):
        a[p, :8] = np.random.permutation(np.resize(levels, 8))
        for g in range(8):
            far = levels[np.abs(levels - a[p, g]) >= 10]
            a[p, g + 8] = far[np.random.randint(len(far))]
    return np.exp2(a.ravel()).repeat(32)


BF16 = ml_dtypes.bfloat16


def bf(x):
    return np.asarray(x, np.float32).astype(BF16)


def f64(x):
    return np.asarray(x).astype(np.float64)


E2M1 = np.array([0.0, 0.5, 1.0, 1.5, 2.0, 3.0, 4.0, 6.0, -0.0, -0.5, -1.0, -1.5, -2.0, -3.0, -4.0, -6.0])


def pack_weight(w, fmt):
    k, n = w.shape
    w = f64(bf(w)).reshape(k // 32, 32, n)
    amax = np.abs(w).max(1)
    if fmt == "e4m3":
        byte = np.frexp(amax)[1] - 1 + 127 - 7
    else:
        mant, ex = np.frexp(amax / 6.0)
        byte = np.where(mant > 0.5, ex, ex - 1) + 127
    byte = np.clip(np.where(amax > 0, byte, 1), 1, 254)
    scaled = (w * np.exp2(127.0 - byte)[:, None, :]).reshape(k, n).astype(np.float32)
    by_word = np.ascontiguousarray(scaled.reshape(k // 512, 128, 4, n).transpose(0, 1, 3, 2))
    if fmt == "e4m3":
        words = by_word.astype(ml_dtypes.float8_e4m3fn).view(np.uint8)
    else:
        c = by_word.astype(ml_dtypes.float4_e2m1fn).view(np.uint8) & 0xF
        words = c[..., 0::2] | (c[..., 1::2] << 4)
    return np.ascontiguousarray(words), np.ascontiguousarray(byte.astype(np.uint8).reshape(k // 512, 16, n))


def unpack_weight(words, scales, fmt):
    g, p, n, _ = words.shape
    if fmt == "e4m3":
        vals = np.ascontiguousarray(words).view(ml_dtypes.float8_e4m3fn).astype(np.float64)
    else:
        nib = np.empty((g, p, n, 4), np.uint8)
        nib[..., 0::2] = words & 0xF
        nib[..., 1::2] = words >> 4
        vals = E2M1[nib]
    vals = vals * np.repeat(np.exp2(scales.astype(np.float64) - 127.0), 8, axis=1)[..., None]
    return vals.transpose(0, 1, 3, 2).reshape(g * 512, n)

def pack4(w):
    words, scales = pack_weight(w, "e2m1")
    return words.reshape(words.shape[0], 128, -1), scales


def unpack4(words, scales):
    return unpack_weight(words.reshape(words.shape[0], 128, -1, 2), scales, "e2m1")


B, N, D, H, DK, DV = 4, 1024, 512, 8, 64, 64


def xnorm(x, g):
    n = np.sqrt(np.sum(x * x, axis=-1, keepdims=True))
    return x * g / n


def setup_inputs():
    s = mx_kscale(D)
    queries = bf(np.random.standard_normal((B, N, D)) * s)
    Wq_words, Wq_scales = pack4(np.random.standard_normal((D, H * DK)) / np.sqrt(D) / s[:, None])
    return {
        "queries": queries,
        "Wq_words": Wq_words,
        "Wq_scales": Wq_scales,
        "bq": bf(np.random.standard_normal(H * DK) * 0.1),
        "gamma": bf(np.random.standard_normal((1, H, 1, 1)) * 2.0),
    }


def reference(queries, Wq_words, Wq_scales, bq, gamma):
    q = ((mxq(f64(queries), 2, "e5m2") @ unpack4(Wq_words, Wq_scales)) + f64(bq)).reshape(B, N, H, DK)
    return xnorm(q.transpose(0, 2, 1, 3), f64(gamma))

@@ -1,0 +1,229 @@
+from contextlib import ExitStack
+
+import concourse.mybir as mybir
+from concourse.masks import make_identity
+
+B, N, D, H, DK = 4, 1024, 512, 8, 64
+FLOPS = 2 * B * N * D * H * DK
+
+F32 = mybir.dt.float32
+BF16 = mybir.dt.bfloat16
+I32 = mybir.dt.int32
+U32 = mybir.dt.uint32
+U8 = mybir.dt.uint8
+E5M2 = mybir.dt.float8_e5m2_x4
+E2M1 = mybir.dt.float4_e2m1fn_x4
+ACT = mybir.ActivationFunctionType
+ALU = mybir.AluOpType
+AX = mybir.AxisListType
+
+P = 128
+J = 4
+G = B * N // (P * J)
+HB = [4,3,4,3,4,3,4,3]
+HC = [6,6,6,6,6,6,5,0]
+LAST_DVE = 5
+
+
+def tile_ufoattention_pb_kernel(tc, queries, Wq_words, Wq_scales, bq, gamma, out):
+    nc = tc.nc
+    xg = queries.rearrange("b (u p j) k -> (b u) p j k", p=P, j=J)
+    og = out.rearrange("b h (u p j) d -> b u p h (j d)", p=P, j=J)
+
+    with ExitStack() as ctx:
+        keep = ctx.enter_context(tc.tile_pool(name="keep", bufs=1))
+        tp = ctx.enter_context(tc.psum_pool(name="tp", bufs=2))
+        accp = ctx.enter_context(tc.psum_pool(name="accp", bufs=5))
+        gp = ctx.enter_context(tc.psum_pool(name="gp", bufs=1))
+        ctx.enter_context(tc.manual_schedule())
+
+        def sb(name, shape, dtype):
+            return keep.tile(shape, dtype, name=name, align_bytes=64)
+
+        ident = sb("ident", [P, P], F32)
+        ones = sb("ones", [P, P], BF16)
+        rows = sb("rows", [P, D + 32], BF16)
+        w_words = sb("w_words", [P, 2 * D], U8)
+        w_plane = sb("w_plane", [P, D], U8)
+        bias = sb("bias", [P, D], F32)
+        x = [[sb("x%d_%d" % (g, a), [P, 2, D], BF16) for a in range(2)] if g == 0 else sb("x%d" % g, [P, J, D], BF16) for g in range(G)]
+        xt = [sb("xt%d" % g, [P, J, P, 4], BF16) for g in range(G)]
+        codes = [sb("codes%d" % g, [P, J * P], U32) for g in range(G)]
+        scales = [sb("scales%d" % g, [P, J * P], U8) for g in range(G)]
+        y = [sb("y%d" % g, [P, J, H, DK], F32) for g in range(G)]
+        o = [sb("o%d" % g, [P, H, J, DK], F32) for g in range(G)]
+        st = [sb("st%d" % g, [P, H, J, 3], F32) for g in range(G)]
+        ss = [sb("ss%d" % g, [P, H, J], F32) for g in range(G)]
+        rs = [sb("rs%d" % g, [P, H, J], F32) for g in range(G)]
+        s = [sb("s%d" % g, [P, H, J], F32) for g in range(G)]
+        gam = gp.tile([P, H], F32, name="gam")
+        tbank = {}
+        acc = {}
+
+        def xpair(g, a):
+            return x[0][a][:] if g == 0 else x[g][:, 2 * a : 2 * a + 2, :]
+
+        def transposes(g, a):
+            bank = tp.tile([P, 2, 2, P], F32, name="tb")
+            tbank[(g, a)] = bank
+            words = xpair(g, a).bitcast(F32)
+            for i in range(2):
+                for u in range(2):
+                    nc.tensor.transpose(bank[:, i, u, :], words[:, i, u : D // 2 : 2], ident[:])
+
+        def copy_out(g, a):
+            nc.scalar.copy(
+                out=xt[g][:, 2 * a : 2 * a + 2, :, :].bitcast(F32),
+                in_=tbank[(g, a)][:].rearrange("p i u r -> p i r u"),
+            )
+
+        def quantize(g, j0, j1):
+            nc.vector.quantize_mx(
+                out=codes[g][:, j0 * P : j1 * P].bitcast(E5M2),
+                scales=scales[g][:, j0 * P : j1 * P],
+                in_=xt[g][:, j0:j1, :, :].rearrange("p j r t -> p (j r t)"),
+            )
+
+        def project(g, j):
+            bank = accp.tile([P, D], F32, name="acc")
+            acc[(g, j)] = bank
+            nc.tensor.matmul_mx(
+                out=bank[:],
+                lhsT=codes[g][:, j * P : (j + 1) * P].bitcast(E5M2),
+                lhsT_scale=scales[g][:, j * P : (j + 1) * P],
+                rhs=w_words[:].bitcast(E2M1),
+                rhs_scale=w_plane[:],
+                start=True,
+                stop=True,
+            )
+
+        def add_bias(g, j):
+            nc.vector.tensor_tensor(out=y[g][:, j, :, :].rearrange("p h d -> p (h d)"), in0=acc[(g, j)][:], in1=bias[:], op=ALU.add)
+
+        def squares(g, j):
+            for h in range(HB[g], H):
+                nc.scalar.activation(out=o[g][:, h, j, :], in_=y[g][:, j, h, :], func=ACT.Square, accum_out=ss[g][:, h, j : j + 1])
+
+        def stats(g, a):
+            for h in range(HB[g]):
+                nc.vector.bn_stats(
+                    out=st[g][:, h, 2 * a : 2 * a + 2, :].rearrange("p j c -> p (j c)"),
+                    in_=y[g][:, 2 * a : 2 * a + 2, h, :].rearrange("p j d -> p d j"),
+                )
+
+        def mean_sq(g):
+            v = st[g][:, 0 : HB[g], :, :]
+            nc.scalar.activation(out=v[:, :, :, 0], in_=v[:, :, :, 1], func=ACT.Square, scale=8.0)
+
+        def join(g):
+            nc.vector.tensor_reduce(
+                out=ss[g][:, 0 : HB[g], :].rearrange("p h j -> p (h j)"),
+                in_=st[g][:, 0 : HB[g], :, 0:3:2].rearrange("p h j c -> p (h j) c"),
+                axis=AX.X,
+                op=ALU.add,
+            )
+
+        def rsqrt(g):
+            nc.scalar.activation(out=rs[g][:], in_=ss[g][:], func=ACT.Abs_reciprocal_sqrt)
+
+        def gain(g):
+            nc.vector.tensor_tensor(out=s[g][:], in0=gam[:].unsqueeze(2).to_broadcast([P, H, J]), in1=rs[g][:], op=ALU.mult)
+
+        def scale_wide(eng, g, h0, h1):
+            eng.tensor_tensor(
+                out=o[g][:, h0:h1, :, :],
+                in0=y[g][:, :, h0:h1, :].rearrange("p j h d -> p h j d"),
+                in1=s[g][:, h0:h1, :].unsqueeze(3).to_broadcast([P, h1 - h0, J, DK]),
+                op=ALU.mult,
+            )
+
+        def scale_act(g, h0, h1):
+            for h in range(h0, h1):
+                for j in range(J):
+                    nc.scalar.activation(out=o[g][:, h, j, :], in_=y[g][:, j, h, :], func=ACT.Copy, scale=s[g][:, h, j : j + 1])
+
+        def store(g, h0, h1):
+            nc.sync.dma_start(out=og[g // 2, g % 2, :, h0:h1, :], in_=o[g][:, h0:h1, :, :].rearrange("p h j d -> p h (j d)"))
+
+        nc.sync.dma_start(out=x[0][0][:], in_=xg[0, :, 0:2, :])
+        nc.sync.dma_start(out=w_words[:].bitcast(I32), in_=Wq_words[0].bitcast(I32))
+        nc.sync.dma_start(out=x[0][1][:], in_=xg[0, :, 2:4, :])
+        for g in range(1, G):
+            nc.sync.dma_start(out=x[g][:], in_=xg[g])
+        nc.vector.memset(rows[:].bitcast(I32), 0)
+        nc.vector.memset(w_plane[:].bitcast(I32), 0)
+        nc.vector.memset(ones[:], 1.0)
+        make_identity(nc, ident[:])
+        nc.scalar.dma_start(out=rows[0:1, 0:D], in_=bq.rearrange("(o n) -> o n", o=1))
+        nc.scalar.dma_start(out=rows[0:1, D : D + H], in_=gamma.rearrange("a h b c -> a (h b c)"))
+        for q in range(4):
+            nc.scalar.dma_start(out=w_plane[32 * q : 32 * q + 4, :].bitcast(I32), in_=Wq_scales[0, 4 * q : 4 * q + 4, :].bitcast(I32))
+
+        transposes(0, 0)
+        bias_bank = accp.tile([P, D], F32, name="acc")
+        nc.tensor.matmul(bias_bank[:], ones[:], rows[:, 0:D], start=True, stop=True)
+        nc.tensor.matmul(gam[:], ones[:], rows[:, D : D + H], start=True, stop=True)
+        copy_out(0, 0)
+        transposes(0, 1)
+        quantize(0, 0, 2)
+        nc.vector.tensor_copy(out=bias[:], in_=bias_bank[:])
+        copy_out(0, 1)
+        project(0, 0)
+        project(0, 1)
+        quantize(0, 2, 4)
+        transposes(1, 0)
+        transposes(1, 1)
+        project(0, 2)
+        project(0, 3)
+        copy_out(1, 0)
+        copy_out(1, 1)
+
+        for k in range(G):
+            if k + 2 < G:
+                transposes(k + 2, 0)
+                transposes(k + 2, 1)
+            add_bias(k, 0)
+            if k > 0:
+                squares(k - 1, 3)
+            squares(k, 0)
+            if k > 0:
+                stats(k - 1, 1)
+                mean_sq(k - 1)
+            add_bias(k, 1)
+            if k + 2 < G:
+                copy_out(k + 2, 0)
+            if k > 0:
+                join(k - 1)
+                rsqrt(k - 1)
+            add_bias(k, 2)
+            squares(k, 1)
+            if k + 1 < G:
+                quantize(k + 1, 0, J)
+                for j in range(J):
+                    project(k + 1, j)
+            if k > 0:
+                gain(k - 1)
+                scale_wide(nc.gpsimd, k - 1, 0, HC[k - 1])
+            if k + 2 < G:
+                copy_out(k + 2, 1)
+            stats(k, 0)
+            squares(k, 2)
+            if k > 0:
+                scale_act(k - 1, HC[k - 1], H)
+                store(k - 1, HC[k - 1], H)
+                store(k - 1, 0, HC[k - 1])
+            add_bias(k, 3)
+
+        k = G - 1
+        squares(k, 3)
+        stats(k, 1)
+        mean_sq(k)
+        join(k)
+        rsqrt(k)
+        gain(k)
+        scale_wide(nc.vector, k, 0, 2)
+        scale_act(k, LAST_DVE, H)
+        store(k, 0, 2)
+        scale_wide(nc.vector, k, 2, LAST_DVE)
+        store(k, LAST_DVE, H)
+        store(k, 2, LAST_DVE)

@@ -20,9 +20,12 @@ AX = mybir.AxisListType
 P = 128
 J = 4
 G = B * N // (P * J)
-HB = [4,3,4,3,4,3,4,3]
-HC = [6,6,6,6,6,6,5,0]
-LAST_DVE = 5
+UNITS = [[0,8,3,5,0],[1,8,4,5,0],[2,8,4,5,0],[3,8,4,5,0],[4,8,4,5,0],[5,8,4,5,0],[6,4,1,2,0],[6,4,1,2,0],[7,4,2,0,2],[7,4,2,0,2]]
+LAG = [1,2,2,3,0]
+LEAD = [2,6,4,2]
+PER_SLOT = 2
+STORE_LAG = 1
+ACC_BANKS = 5
 
 
 def tile_ufoattention_pb_kernel(tc, queries, Wq_words, Wq_scales, bq, gamma, out):
@@ -46,35 +49,50 @@ def tile_ufoattention_pb_kernel(tc, queries, Wq_words, Wq_scales, bq, gamma, out
         w_words = sb("w_words", [P, 2 * D], U8)
         w_plane = sb("w_plane", [P, D], U8)
         bias = sb("bias", [P, D], F32)
-        x = [[sb("x%d_%d" % (g, a), [P, 2, D], BF16) for a in range(2)] if g == 0 else sb("x%d" % g, [P, J, D], BF16) for g in range(G)]
+        x = [None] + [sb("x%d" % g, [P, J, D], BF16) for g in range(1, G)]
+        x_first = [sb("xa", [P, 1, D], BF16), sb("xb", [P, 3, D], BF16)]
         xt = [sb("xt%d" % g, [P, J, P, 4], BF16) for g in range(G)]
         codes = [sb("codes%d" % g, [P, J * P], U32) for g in range(G)]
         scales = [sb("scales%d" % g, [P, J * P], U8) for g in range(G)]
-        y = [sb("y%d" % g, [P, J, H, DK], F32) for g in range(G)]
-        o = [sb("o%d" % g, [P, H, J, DK], F32) for g in range(G)]
-        st = [sb("st%d" % g, [P, H, J, 3], F32) for g in range(G)]
-        ss = [sb("ss%d" % g, [P, H, J], F32) for g in range(G)]
-        rs = [sb("rs%d" % g, [P, H, J], F32) for g in range(G)]
-        s = [sb("s%d" % g, [P, H, J], F32) for g in range(G)]
         gam = gp.tile([P, H], F32, name="gam")
+
+        banks = []
+        ends = {}
+        head0 = []
+        y, o, st, ss, rs, s = [], [], [], [], [], []
+        for u, (g, nh, hb, hc, hd) in enumerate(UNITS):
+            head0.append(sum(v[1] for v in UNITS[:u] if v[0] == g))
+            per = H // nh
+            for j in range(0, J, per):
+                banks.append((u, j, j + per))
+            ends[len(banks) - 1] = u
+            y.append(sb("y%d" % u, [P, J, nh, DK], F32))
+            o.append(sb("o%d" % u, [P, nh, J, DK], F32))
+            st.append(sb("st%d" % u, [P, nh, J, 3], F32))
+            ss.append(sb("ss%d" % u, [P, nh, J], F32))
+            rs.append(sb("rs%d" % u, [P, nh, J], F32))
+            s.append(sb("s%d" % u, [P, nh, J], F32))
+        NB = len(banks)
         tbank = {}
         acc = {}
+        quantised = set()
+        done = set()
+        t_order = []
 
-        def xpair(g, a):
-            return x[0][a][:] if g == 0 else x[g][:, 2 * a : 2 * a + 2, :]
-
-        def transposes(g, a):
+        def transposes(g, j0, j1, src):
             bank = tp.tile([P, 2, 2, P], F32, name="tb")
-            tbank[(g, a)] = bank
-            words = xpair(g, a).bitcast(F32)
-            for i in range(2):
-                for u in range(2):
-                    nc.tensor.transpose(bank[:, i, u, :], words[:, i, u : D // 2 : 2], ident[:])
+            tbank[(g, j0)] = bank
+            t_order.append((g, j0))
+            words = src.bitcast(F32)
+            for i in range(j1 - j0):
+                for v in range(2):
+                    nc.tensor.transpose(bank[:, i, v, :], words[:, i, v : D // 2 : 2], ident[:])
 
-        def copy_out(g, a):
+        def copy_out(g, j0, j1):
+            done.add(("copy", g, j0))
             nc.scalar.copy(
-                out=xt[g][:, 2 * a : 2 * a + 2, :, :].bitcast(F32),
-                in_=tbank[(g, a)][:].rearrange("p i u r -> p i r u"),
+                out=xt[g][:, j0:j1, :, :].bitcast(F32),
+                in_=tbank[(g, j0)][:, 0 : j1 - j0, :, :].rearrange("p i u r -> p i r u"),
             )
 
         def quantize(g, j0, j1):
@@ -83,147 +101,200 @@ def tile_ufoattention_pb_kernel(tc, queries, Wq_words, Wq_scales, bq, gamma, out
                 scales=scales[g][:, j0 * P : j1 * P],
                 in_=xt[g][:, j0:j1, :, :].rearrange("p j r t -> p (j r t)"),
             )
+            for j in range(j0, j1):
+                quantised.add((g, j))
 
-        def project(g, j):
-            bank = accp.tile([P, D], F32, name="acc")
-            acc[(g, j)] = bank
-            nc.tensor.matmul_mx(
-                out=bank[:],
-                lhsT=codes[g][:, j * P : (j + 1) * P].bitcast(E5M2),
-                lhsT_scale=scales[g][:, j * P : (j + 1) * P],
-                rhs=w_words[:].bitcast(E2M1),
-                rhs_scale=w_plane[:],
-                start=True,
-                stop=True,
-            )
+        waiting = list(range(NB))
 
-        def add_bias(g, j):
-            nc.vector.tensor_tensor(out=y[g][:, j, :, :].rearrange("p h d -> p (h d)"), in0=acc[(g, j)][:], in1=bias[:], op=ALU.add)
+        def project(upto):
+            while waiting and waiting[0] <= upto:
+                u, j0, j1 = banks[waiting[0]]
+                g, nh = UNITS[u][0], UNITS[u][1]
+                if not all((g, j) in quantised for j in range(j0, j1)):
+                    return
+                bank = accp.tile([P, D], F32, name="acc")
+                acc[waiting.pop(0)] = bank
+                c0, w = head0[u] * DK, nh * DK
+                for j in range(j0, j1):
+                    nc.tensor.matmul_mx(
+                        out=bank[:, (j - j0) * w : (j - j0 + 1) * w],
+                        lhsT=codes[g][:, j * P : (j + 1) * P].bitcast(E5M2),
+                        lhsT_scale=scales[g][:, j * P : (j + 1) * P],
+                        rhs=w_words[:, 2 * c0 : 2 * (c0 + w)].bitcast(E2M1),
+                        rhs_scale=w_plane[:, c0 : c0 + w],
+                        start=True,
+                        stop=True,
+                    )
 
-        def squares(g, j):
-            for h in range(HB[g], H):
-                nc.scalar.activation(out=o[g][:, h, j, :], in_=y[g][:, j, h, :], func=ACT.Square, accum_out=ss[g][:, h, j : j + 1])
-
-        def stats(g, a):
-            for h in range(HB[g]):
-                nc.vector.bn_stats(
-                    out=st[g][:, h, 2 * a : 2 * a + 2, :].rearrange("p j c -> p (j c)"),
-                    in_=y[g][:, 2 * a : 2 * a + 2, h, :].rearrange("p j d -> p d j"),
-                )
-
-        def mean_sq(g):
-            v = st[g][:, 0 : HB[g], :, :]
-            nc.scalar.activation(out=v[:, :, :, 0], in_=v[:, :, :, 1], func=ACT.Square, scale=8.0)
-
-        def join(g):
-            nc.vector.tensor_reduce(
-                out=ss[g][:, 0 : HB[g], :].rearrange("p h j -> p (h j)"),
-                in_=st[g][:, 0 : HB[g], :, 0:3:2].rearrange("p h j c -> p (h j) c"),
-                axis=AX.X,
+        def add_bias(n):
+            u, j0, j1 = banks[n]
+            c0, w = head0[u] * DK, UNITS[u][1] * DK
+            nc.vector.tensor_tensor(
+                out=y[u][:, j0:j1, :, :].rearrange("p j h d -> p j (h d)"),
+                in0=acc[n][:].rearrange("p (j c) -> p j c", c=w),
+                in1=bias[:, c0 : c0 + w].unsqueeze(1).to_broadcast([P, j1 - j0, w]),
                 op=ALU.add,
             )
 
-        def rsqrt(g):
-            nc.scalar.activation(out=rs[g][:], in_=ss[g][:], func=ACT.Abs_reciprocal_sqrt)
+        def squares(n):
+            u, j0, j1 = banks[n]
+            for j in range(j0, j1):
+                for h in range(UNITS[u][2], UNITS[u][1]):
+                    nc.scalar.activation(out=o[u][:, h, j, :], in_=y[u][:, j, h, :], func=ACT.Square, accum_out=ss[u][:, h, j : j + 1])
 
-        def gain(g):
-            nc.vector.tensor_tensor(out=s[g][:], in0=gam[:].unsqueeze(2).to_broadcast([P, H, J]), in1=rs[g][:], op=ALU.mult)
+        def stats(n):
+            u, j0, j1 = banks[n]
+            if j1 % 2:
+                return
+            for a in range(j0 // 2, j1 // 2):
+                for h in range(UNITS[u][2]):
+                    nc.vector.bn_stats(
+                        out=st[u][:, h, 2 * a : 2 * a + 2, :].rearrange("p j c -> p (j c)"),
+                        in_=y[u][:, 2 * a : 2 * a + 2, h, :].rearrange("p j d -> p d j"),
+                    )
 
-        def scale_wide(eng, g, h0, h1):
-            eng.tensor_tensor(
-                out=o[g][:, h0:h1, :, :],
-                in0=y[g][:, :, h0:h1, :].rearrange("p j h d -> p h j d"),
-                in1=s[g][:, h0:h1, :].unsqueeze(3).to_broadcast([P, h1 - h0, J, DK]),
-                op=ALU.mult,
+        def mean_sq(u):
+            if UNITS[u][2]:
+                v = st[u][:, 0 : UNITS[u][2], :, :]
+                nc.scalar.activation(out=v[:, :, :, 0], in_=v[:, :, :, 1], func=ACT.Square, scale=8.0)
+
+        def join(u):
+            hb = UNITS[u][2]
+            if hb:
+                nc.vector.tensor_reduce(
+                    out=ss[u][:, 0:hb, :].rearrange("p h j -> p (h j)"),
+                    in_=st[u][:, 0:hb, :, 0:3:2].rearrange("p h j c -> p (h j) c"),
+                    axis=AX.X,
+                    op=ALU.add,
+                )
+
+        def rsqrt(u):
+            nc.scalar.activation(out=rs[u][:], in_=ss[u][:], func=ACT.Abs_reciprocal_sqrt)
+
+        def gain(u):
+            nh = UNITS[u][1]
+            nc.vector.tensor_tensor(
+                out=s[u][:], in0=gam[:, head0[u] : head0[u] + nh].unsqueeze(2).to_broadcast([P, nh, J]), in1=rs[u][:], op=ALU.mult
             )
 
-        def scale_act(g, h0, h1):
-            for h in range(h0, h1):
-                for j in range(J):
-                    nc.scalar.activation(out=o[g][:, h, j, :], in_=y[g][:, j, h, :], func=ACT.Copy, scale=s[g][:, h, j : j + 1])
+        def scale_wide(eng, u, h0, h1):
+            if h1 > h0:
+                eng.tensor_tensor(
+                    out=o[u][:, h0:h1, :, :],
+                    in0=y[u][:, :, h0:h1, :].rearrange("p j h d -> p h j d"),
+                    in1=s[u][:, h0:h1, :].unsqueeze(3).to_broadcast([P, h1 - h0, J, DK]),
+                    op=ALU.mult,
+                )
 
-        def store(g, h0, h1):
-            nc.sync.dma_start(out=og[g // 2, g % 2, :, h0:h1, :], in_=o[g][:, h0:h1, :, :].rearrange("p h j d -> p h (j d)"))
+        def scale_act(u, h):
+            for j in range(J):
+                nc.scalar.activation(out=o[u][:, h, j, :], in_=y[u][:, j, h, :], func=ACT.Copy, scale=s[u][:, h, j : j + 1])
 
-        nc.sync.dma_start(out=x[0][0][:], in_=xg[0, :, 0:2, :])
-        nc.sync.dma_start(out=w_words[:].bitcast(I32), in_=Wq_words[0].bitcast(I32))
-        nc.sync.dma_start(out=x[0][1][:], in_=xg[0, :, 2:4, :])
-        for g in range(1, G):
-            nc.sync.dma_start(out=x[g][:], in_=xg[g])
-        nc.vector.memset(rows[:].bitcast(I32), 0)
+        def store(u, h0, h1):
+            if h1 > h0:
+                g = UNITS[u][0]
+                nc.sync.dma_start(
+                    out=og[g // 2, g % 2, :, head0[u] + h0 : head0[u] + h1, :],
+                    in_=o[u][:, h0:h1, :, :].rearrange("p h j d -> p h (j d)"),
+                )
+
+        l1, l2, l3, l4, lc = LAG
+        le, ld0, ld1, lt = LEAD
+
+        def front(n):
+            for g in range(1, G):
+                for j0, ld in ((0, ld0), (2, ld1)):
+                    if J * g - ld - lt <= n and (g, j0) not in tbank and ("copy",) + t_order[-2] in done:
+                        transposes(g, j0, j0 + 2, x[g][:, j0 : j0 + 2, :])
+
+        def copies(n):
+            for g in range(1, G):
+                for j0, ld in ((0, ld0), (2, ld1)):
+                    if J * g - ld <= n and ("copy", g, j0) not in done:
+                        front(n)
+                        copy_out(g, j0, j0 + 2)
+
+        def quant(n):
+            for g in range(1, G):
+                if J * g - le <= n and (g, 0) not in quantised:
+                    quantize(g, 0, J)
+                    project(n + ACC_BANKS)
+
         nc.vector.memset(w_plane[:].bitcast(I32), 0)
+        nc.vector.memset(rows[:].bitcast(I32), 0)
         nc.vector.memset(ones[:], 1.0)
         make_identity(nc, ident[:])
-        nc.scalar.dma_start(out=rows[0:1, 0:D], in_=bq.rearrange("(o n) -> o n", o=1))
-        nc.scalar.dma_start(out=rows[0:1, D : D + H], in_=gamma.rearrange("a h b c -> a (h b c)"))
+        nc.sync.dma_start(out=x_first[0][:], in_=xg[0, :, 0:1, :])
+        nc.sync.dma_start(out=w_words[:].bitcast(I32), in_=Wq_words[0].bitcast(I32))
+        nc.sync.dma_start(out=x_first[1][:], in_=xg[0, :, 1:4, :])
         for q in range(4):
             nc.scalar.dma_start(out=w_plane[32 * q : 32 * q + 4, :].bitcast(I32), in_=Wq_scales[0, 4 * q : 4 * q + 4, :].bitcast(I32))
+        nc.scalar.dma_start(out=rows[0:1, 0:D], in_=bq.rearrange("(o n) -> o n", o=1))
+        nc.gpsimd.dma_start(out=rows[0:1, D : D + H], in_=gamma.rearrange("a h b c -> a (h b c)"))
+        for g in range(1, G):
+            nc.sync.dma_start(out=x[g][:], in_=xg[g])
 
-        transposes(0, 0)
+        transposes(0, 0, 1, x_first[0][:])
         bias_bank = accp.tile([P, D], F32, name="acc")
         nc.tensor.matmul(bias_bank[:], ones[:], rows[:, 0:D], start=True, stop=True)
-        nc.tensor.matmul(gam[:], ones[:], rows[:, D : D + H], start=True, stop=True)
-        copy_out(0, 0)
-        transposes(0, 1)
-        quantize(0, 0, 2)
+        transposes(0, 1, 2, x_first[1][:, 0:1, :])
+        copy_out(0, 0, 1)
+        copy_out(0, 1, 2)
+        quantize(0, 0, 1)
         nc.vector.tensor_copy(out=bias[:], in_=bias_bank[:])
-        copy_out(0, 1)
-        project(0, 0)
-        project(0, 1)
+        quantize(0, 1, 2)
+        project(0)
+        transposes(0, 2, 4, x_first[1][:, 1:3, :])
+        project(1)
+        copy_out(0, 2, 4)
+        front(-2)
+        add_bias(0)
         quantize(0, 2, 4)
-        transposes(1, 0)
-        transposes(1, 1)
-        project(0, 2)
-        project(0, 3)
-        copy_out(1, 0)
-        copy_out(1, 1)
+        project(3)
+        nc.tensor.matmul(gam[:], ones[:], rows[:, D : D + H], start=True, stop=True)
+        copies(-1)
+        front(-1)
 
-        for k in range(G):
-            if k + 2 < G:
-                transposes(k + 2, 0)
-                transposes(k + 2, 1)
-            add_bias(k, 0)
-            if k > 0:
-                squares(k - 1, 3)
-            squares(k, 0)
-            if k > 0:
-                stats(k - 1, 1)
-                mean_sq(k - 1)
-            add_bias(k, 1)
-            if k + 2 < G:
-                copy_out(k + 2, 0)
-            if k > 0:
-                join(k - 1)
-                rsqrt(k - 1)
-            add_bias(k, 2)
-            squares(k, 1)
-            if k + 1 < G:
-                quantize(k + 1, 0, J)
-                for j in range(J):
-                    project(k + 1, j)
-            if k > 0:
-                gain(k - 1)
-                scale_wide(nc.gpsimd, k - 1, 0, HC[k - 1])
-            if k + 2 < G:
-                copy_out(k + 2, 1)
-            stats(k, 0)
-            squares(k, 2)
-            if k > 0:
-                scale_act(k - 1, HC[k - 1], H)
-                store(k - 1, HC[k - 1], H)
-                store(k - 1, 0, HC[k - 1])
-            add_bias(k, 3)
-
-        k = G - 1
-        squares(k, 3)
-        stats(k, 1)
-        mean_sq(k)
-        join(k)
-        rsqrt(k)
-        gain(k)
-        scale_wide(nc.vector, k, 0, 2)
-        scale_act(k, LAST_DVE, H)
-        store(k, 0, 2)
-        scale_wide(nc.vector, k, 2, LAST_DVE)
-        store(k, LAST_DVE, H)
-        store(k, 2, LAST_DVE)
+        act_jobs = []
+        late_stores = []
+        for n in range(NB + 8):
+            front(n)
+            if 0 < n < NB:
+                add_bias(n)
+            if n < NB:
+                project(n + ACC_BANKS)
+            late = n - l1 not in ends
+            if 0 < n <= NB:
+                squares(n - 1)
+                if not late:
+                    stats(n - 1)
+            if n - l1 in ends:
+                mean_sq(ends[n - l1])
+            if n - l2 in ends:
+                join(ends[n - l2])
+            if n - l3 in ends:
+                rsqrt(ends[n - l3])
+            copies(n)
+            quant(n)
+            if n - l4 in ends:
+                u = ends[n - l4]
+                g, nh, hb, hc, hd = UNITS[u]
+                gain(u)
+                scale_wide(nc.gpsimd, u, 0, hc)
+                scale_wide(nc.vector, u, hc, hc + hd)
+                for h in range(hc + hd, nh):
+                    act_jobs.append((u, h, n + lc))
+                store(u, hc, hc + hd)
+                late_stores.append((n + STORE_LAG, u, hc))
+            if 0 < n <= NB and late:
+                stats(n - 1)
+            for i in range(len(act_jobs) if n >= NB + 2 else min(len(act_jobs), PER_SLOT)):
+                if act_jobs[0][2] > n and n < NB:
+                    break
+                u, h, t = act_jobs.pop(0)
+                scale_act(u, h)
+                if h == UNITS[u][1] - 1:
+                    store(u, UNITS[u][3] + UNITS[u][4], UNITS[u][1])
+            while late_stores and (late_stores[0][0] <= n or n == NB + 7):
+                t, u, hc = late_stores.pop(0)
+                store(u, 0, hc)

@@ -20,7 +20,7 @@ AX = mybir.AxisListType
 P = 128
 J = 4
 G = B * N // (P * J)
-UNITS = [[0,8,3,5,0],[1,8,4,5,0],[2,8,4,5,0],[3,8,4,5,0],[4,8,4,5,0],[5,8,4,5,0],[6,4,1,2,0],[6,4,1,2,0],[7,4,2,0,2],[7,4,2,0,2]]
+UNITS = [[0,8,3,6,0],[1,8,4,6,0],[2,8,4,6,0],[3,8,4,6,0],[4,8,4,6,0],[5,8,4,6,0],[6,4,1,2,0],[6,4,1,2,0],[7,4,2,0,2],[7,4,2,0,2]]
 LAG = [1,2,2,3,0]
 LEAD = [2,6,4,2]
 PER_SLOT = 2

from contextlib import ExitStack

import concourse.mybir as mybir
from concourse.masks import make_identity

B, N, D, H, DK = 4, 1024, 512, 8, 64
FLOPS = 2 * B * N * D * H * DK

F32 = mybir.dt.float32
BF16 = mybir.dt.bfloat16
I32 = mybir.dt.int32
U32 = mybir.dt.uint32
U8 = mybir.dt.uint8
E5M2 = mybir.dt.float8_e5m2_x4
E2M1 = mybir.dt.float4_e2m1fn_x4
ACT = mybir.ActivationFunctionType
ALU = mybir.AluOpType
AX = mybir.AxisListType

P = 128
J = 4
G = B * N // (P * J)
UNITS = [[0,8,3,6,0],[1,8,4,6,0],[2,8,4,6,0],[3,8,4,6,0],[4,8,4,6,0],[5,8,4,6,0],[6,4,1,2,0],[6,4,1,2,0],[7,4,2,0,2],[7,4,2,0,2]]
LAG = [1,2,2,3,0]
LEAD = [2,6,4,2]
PER_SLOT = 2
STORE_LAG = 1
ACC_BANKS = 5


def tile_ufoattention_pb_kernel(tc, queries, Wq_words, Wq_scales, bq, gamma, out):
    nc = tc.nc
    xg = queries.rearrange("b (u p j) k -> (b u) p j k", p=P, j=J)
    og = out.rearrange("b h (u p j) d -> b u p h (j d)", p=P, j=J)

    with ExitStack() as ctx:
        keep = ctx.enter_context(tc.tile_pool(name="keep", bufs=1))
        tp = ctx.enter_context(tc.psum_pool(name="tp", bufs=2))
        accp = ctx.enter_context(tc.psum_pool(name="accp", bufs=5))
        gp = ctx.enter_context(tc.psum_pool(name="gp", bufs=1))
        ctx.enter_context(tc.manual_schedule())

        def sb(name, shape, dtype):
            return keep.tile(shape, dtype, name=name, align_bytes=64)

        ident = sb("ident", [P, P], F32)
        ones = sb("ones", [P, P], BF16)
        rows = sb("rows", [P, D + 32], BF16)
        w_words = sb("w_words", [P, 2 * D], U8)
        w_plane = sb("w_plane", [P, D], U8)
        bias = sb("bias", [P, D], F32)
        x = [None] + [sb("x%d" % g, [P, J, D], BF16) for g in range(1, G)]
        x_first = [sb("xa", [P, 1, D], BF16), sb("xb", [P, 3, D], BF16)]
        xt = [sb("xt%d" % g, [P, J, P, 4], BF16) for g in range(G)]
        codes = [sb("codes%d" % g, [P, J * P], U32) for g in range(G)]
        scales = [sb("scales%d" % g, [P, J * P], U8) for g in range(G)]
        gam = gp.tile([P, H], F32, name="gam")

        banks = []
        ends = {}
        head0 = []
        y, o, st, ss, rs, s = [], [], [], [], [], []
        for u, (g, nh, hb, hc, hd) in enumerate(UNITS):
            head0.append(sum(v[1] for v in UNITS[:u] if v[0] == g))
            per = H // nh
            for j in range(0, J, per):
                banks.append((u, j, j + per))
            ends[len(banks) - 1] = u
            y.append(sb("y%d" % u, [P, J, nh, DK], F32))
            o.append(sb("o%d" % u, [P, nh, J, DK], F32))
            st.append(sb("st%d" % u, [P, nh, J, 3], F32))
            ss.append(sb("ss%d" % u, [P, nh, J], F32))
            rs.append(sb("rs%d" % u, [P, nh, J], F32))
            s.append(sb("s%d" % u, [P, nh, J], F32))
        NB = len(banks)
        tbank = {}
        acc = {}
        quantised = set()
        done = set()
        t_order = []

        def transposes(g, j0, j1, src):
            bank = tp.tile([P, 2, 2, P], F32, name="tb")
            tbank[(g, j0)] = bank
            t_order.append((g, j0))
            words = src.bitcast(F32)
            for i in range(j1 - j0):
                for v in range(2):
                    nc.tensor.transpose(bank[:, i, v, :], words[:, i, v : D // 2 : 2], ident[:])

        def copy_out(g, j0, j1):
            done.add(("copy", g, j0))
            nc.scalar.copy(
                out=xt[g][:, j0:j1, :, :].bitcast(F32),
                in_=tbank[(g, j0)][:, 0 : j1 - j0, :, :].rearrange("p i u r -> p i r u"),
            )

        def quantize(g, j0, j1):
            nc.vector.quantize_mx(
                out=codes[g][:, j0 * P : j1 * P].bitcast(E5M2),
                scales=scales[g][:, j0 * P : j1 * P],
                in_=xt[g][:, j0:j1, :, :].rearrange("p j r t -> p (j r t)"),
            )
            for j in range(j0, j1):
                quantised.add((g, j))

        waiting = list(range(NB))

        def project(upto):
            while waiting and waiting[0] <= upto:
                u, j0, j1 = banks[waiting[0]]
                g, nh = UNITS[u][0], UNITS[u][1]
                if not all((g, j) in quantised for j in range(j0, j1)):
                    return
                bank = accp.tile([P, D], F32, name="acc")
                acc[waiting.pop(0)] = bank
                c0, w = head0[u] * DK, nh * DK
                for j in range(j0, j1):
                    nc.tensor.matmul_mx(
                        out=bank[:, (j - j0) * w : (j - j0 + 1) * w],
                        lhsT=codes[g][:, j * P : (j + 1) * P].bitcast(E5M2),
                        lhsT_scale=scales[g][:, j * P : (j + 1) * P],
                        rhs=w_words[:, 2 * c0 : 2 * (c0 + w)].bitcast(E2M1),
                        rhs_scale=w_plane[:, c0 : c0 + w],
                        start=True,
                        stop=True,
                    )

        def add_bias(n):
            u, j0, j1 = banks[n]
            c0, w = head0[u] * DK, UNITS[u][1] * DK
            nc.vector.tensor_tensor(
                out=y[u][:, j0:j1, :, :].rearrange("p j h d -> p j (h d)"),
                in0=acc[n][:].rearrange("p (j c) -> p j c", c=w),
                in1=bias[:, c0 : c0 + w].unsqueeze(1).to_broadcast([P, j1 - j0, w]),
                op=ALU.add,
            )

        def squares(n):
            u, j0, j1 = banks[n]
            for j in range(j0, j1):
                for h in range(UNITS[u][2], UNITS[u][1]):
                    nc.scalar.activation(out=o[u][:, h, j, :], in_=y[u][:, j, h, :], func=ACT.Square, accum_out=ss[u][:, h, j : j + 1])

        def stats(n):
            u, j0, j1 = banks[n]
            if j1 % 2:
                return
            for a in range(j0 // 2, j1 // 2):
                for h in range(UNITS[u][2]):
                    nc.vector.bn_stats(
                        out=st[u][:, h, 2 * a : 2 * a + 2, :].rearrange("p j c -> p (j c)"),
                        in_=y[u][:, 2 * a : 2 * a + 2, h, :].rearrange("p j d -> p d j"),
                    )

        def mean_sq(u):
            if UNITS[u][2]:
                v = st[u][:, 0 : UNITS[u][2], :, :]
                nc.scalar.activation(out=v[:, :, :, 0], in_=v[:, :, :, 1], func=ACT.Square, scale=8.0)

        def join(u):
            hb = UNITS[u][2]
            if hb:
                nc.vector.tensor_reduce(
                    out=ss[u][:, 0:hb, :].rearrange("p h j -> p (h j)"),
                    in_=st[u][:, 0:hb, :, 0:3:2].rearrange("p h j c -> p (h j) c"),
                    axis=AX.X,
                    op=ALU.add,
                )

        def rsqrt(u):
            nc.scalar.activation(out=rs[u][:], in_=ss[u][:], func=ACT.Abs_reciprocal_sqrt)

        def gain(u):
            nh = UNITS[u][1]
            nc.vector.tensor_tensor(
                out=s[u][:], in0=gam[:, head0[u] : head0[u] + nh].unsqueeze(2).to_broadcast([P, nh, J]), in1=rs[u][:], op=ALU.mult
            )

        def scale_wide(eng, u, h0, h1):
            if h1 > h0:
                eng.tensor_tensor(
                    out=o[u][:, h0:h1, :, :],
                    in0=y[u][:, :, h0:h1, :].rearrange("p j h d -> p h j d"),
                    in1=s[u][:, h0:h1, :].unsqueeze(3).to_broadcast([P, h1 - h0, J, DK]),
                    op=ALU.mult,
                )

        def scale_act(u, h):
            for j in range(J):
                nc.scalar.activation(out=o[u][:, h, j, :], in_=y[u][:, j, h, :], func=ACT.Copy, scale=s[u][:, h, j : j + 1])

        def store(u, h0, h1):
            if h1 > h0:
                g = UNITS[u][0]
                nc.sync.dma_start(
                    out=og[g // 2, g % 2, :, head0[u] + h0 : head0[u] + h1, :],
                    in_=o[u][:, h0:h1, :, :].rearrange("p h j d -> p h (j d)"),
                )

        l1, l2, l3, l4, lc = LAG
        le, ld0, ld1, lt = LEAD

        def front(n):
            for g in range(1, G):
                for j0, ld in ((0, ld0), (2, ld1)):
                    if J * g - ld - lt <= n and (g, j0) not in tbank and ("copy",) + t_order[-2] in done:
                        transposes(g, j0, j0 + 2, x[g][:, j0 : j0 + 2, :])

        def copies(n):
            for g in range(1, G):
                for j0, ld in ((0, ld0), (2, ld1)):
                    if J * g - ld <= n and ("copy", g, j0) not in done:
                        front(n)
                        copy_out(g, j0, j0 + 2)

        def quant(n):
            for g in range(1, G):
                if J * g - le <= n and (g, 0) not in quantised:
                    quantize(g, 0, J)
                    project(n + ACC_BANKS)

        nc.vector.memset(w_plane[:].bitcast(I32), 0)
        nc.vector.memset(rows[:].bitcast(I32), 0)
        nc.vector.memset(ones[:], 1.0)
        make_identity(nc, ident[:])
        nc.sync.dma_start(out=x_first[0][:], in_=xg[0, :, 0:1, :])
        nc.sync.dma_start(out=w_words[:].bitcast(I32), in_=Wq_words[0].bitcast(I32))
        nc.sync.dma_start(out=x_first[1][:], in_=xg[0, :, 1:4, :])
        for q in range(4):
            nc.scalar.dma_start(out=w_plane[32 * q : 32 * q + 4, :].bitcast(I32), in_=Wq_scales[0, 4 * q : 4 * q + 4, :].bitcast(I32))
        nc.scalar.dma_start(out=rows[0:1, 0:D], in_=bq.rearrange("(o n) -> o n", o=1))
        nc.gpsimd.dma_start(out=rows[0:1, D : D + H], in_=gamma.rearrange("a h b c -> a (h b c)"))
        for g in range(1, G):
            nc.sync.dma_start(out=x[g][:], in_=xg[g])

        transposes(0, 0, 1, x_first[0][:])
        bias_bank = accp.tile([P, D], F32, name="acc")
        nc.tensor.matmul(bias_bank[:], ones[:], rows[:, 0:D], start=True, stop=True)
        transposes(0, 1, 2, x_first[1][:, 0:1, :])
        copy_out(0, 0, 1)
        copy_out(0, 1, 2)
        quantize(0, 0, 1)
        nc.vector.tensor_copy(out=bias[:], in_=bias_bank[:])
        quantize(0, 1, 2)
        project(0)
        transposes(0, 2, 4, x_first[1][:, 1:3, :])
        project(1)
        copy_out(0, 2, 4)
        front(-2)
        add_bias(0)
        quantize(0, 2, 4)
        project(3)
        nc.tensor.matmul(gam[:], ones[:], rows[:, D : D + H], start=True, stop=True)
        copies(-1)
        front(-1)

        act_jobs = []
        late_stores = []
        for n in range(NB + 8):
            front(n)
            if 0 < n < NB:
                add_bias(n)
            if n < NB:
                project(n + ACC_BANKS)
            late = n - l1 not in ends
            if 0 < n <= NB:
                squares(n - 1)
                if not late:
                    stats(n - 1)
            if n - l1 in ends:
                mean_sq(ends[n - l1])
            if n - l2 in ends:
                join(ends[n - l2])
            if n - l3 in ends:
                rsqrt(ends[n - l3])
            copies(n)
            quant(n)
            if n - l4 in ends:
                u = ends[n - l4]
                g, nh, hb, hc, hd = UNITS[u]
                gain(u)
                scale_wide(nc.gpsimd, u, 0, hc)
                scale_wide(nc.vector, u, hc, hc + hd)
                for h in range(hc + hd, nh):
                    act_jobs.append((u, h, n + lc))
                store(u, hc, hc + hd)
                late_stores.append((n + STORE_LAG, u, hc))
            if 0 < n <= NB and late:
                stats(n - 1)
            for i in range(len(act_jobs) if n >= NB + 2 else min(len(act_jobs), PER_SLOT)):
                if act_jobs[0][2] > n and n < NB:
                    break
                u, h, t = act_jobs.pop(0)
                scale_act(u, h)
                if h == UNITS[u][1] - 1:
                    store(u, UNITS[u][3] + UNITS[u][4], UNITS[u][1])
            while late_stores and (late_stores[0][0] <= n or n == NB + 7):
                t, u, hc = late_stores.pop(0)
                store(u, 0, hc)
